import numpy as np
import ml_dtypes


def mxq(x, axis, fmt="e4m3"):
    dtype, down = {"e4m3": (ml_dtypes.float8_e4m3fn, 7), "e5m2": (ml_dtypes.float8_e5m2, 14)}[fmt]
    v = np.moveaxis(np.asarray(x, np.float32).astype(ml_dtypes.bfloat16).astype(np.float64), axis, -1)
    blocks = v.reshape(v.shape[:-1] + (-1, 32))
    amax = np.abs(blocks).max(-1, keepdims=True)
    byte = np.maximum(np.where(amax > 0, np.frexp(amax)[1] - 1 + 127, 0) - down, 1)
    scale = np.exp2(byte - 127.0)
    codes = (blocks / scale).astype(np.float32).astype(dtype).astype(np.float64)
    return np.moveaxis((codes * scale).reshape(v.shape), -1, axis)


WIDE = False


def mx_kscale(k):
    if not WIDE:
        return np.ones(k)
    levels = np.array([10, -10, 5, -5, 0])
    a = np.random.permutation(np.resize(levels, k // 512 * 4)).reshape(k // 512, 4)
    idx = np.arange(k)
    return np.exp2(a[idx // 512, idx % 128 // 32])


BF16 = ml_dtypes.bfloat16


def bf(x):
    return np.asarray(x, np.float32).astype(BF16)


def f64(x):
    return np.asarray(x).astype(np.float64)


B, N, F, O, E, K = 4, 512, 512, 64, 16, 3


def normalize_adj(a):
    a = np.maximum(a, 0.0) + np.eye(N)[None, :, :]
    d = np.maximum(a.sum(-1), 1e-6)
    r = d ** -0.5
    return r[:, :, None] * a * r[:, None, :]


def setup_inputs():
    s = mx_kscale(N)
    u = (s / s.min()) ** 2
    x = 0.7 * np.random.standard_normal((B, N, F)) + 0.7 * np.random.standard_normal((B, 1, F))
    x = x * (s / s.max())[None, :, None]
    a0 = 0.5 * (np.random.standard_normal((B, N, N)) - 1.0)
    a = u[None, :, None] * a0
    i = np.arange(N)
    a[:, i, i] = u[None, :] * (np.maximum(a0[:, i, i], 0.0) + 1.0) - 1.0
    return {"A": bf(a), "x": bf(x)}


def reference(A, x):
    a_hat = normalize_adj(f64(A))
    a_left = mxq(a_hat, 2, "e4m3")
    xq = mxq(f64(x), 1, "e4m3")
    t2 = 2.0 * (a_left @ mxq(a_hat, 1, "e4m3")) - np.eye(N)[None, :, :]
    xg1 = a_left @ xq
    xg2 = mxq(t2, 2, "e4m3") @ xq
    return np.stack([xg1, xg2], axis=1)

@@ -1,0 +1,180 @@
+from contextlib import ExitStack
+
+import concourse.mybir as mybir
+from concourse.masks import make_identity
+
+BF16 = mybir.dt.bfloat16
+F32 = mybir.dt.float32
+U32 = mybir.dt.uint32
+U8 = mybir.dt.uint8
+FP8X4 = mybir.dt.float8_e4m3fn_x4
+ACT = mybir.ActivationFunctionType
+ALU = mybir.AluOpType
+
+P = 128
+PACK = 4
+GRAPHS = 4
+NODES = P * PACK
+FEATS = 512
+DIAG_STEP = NODES + P
+
+FLOPS = 3 * GRAPHS * 2 * NODES * NODES * FEATS
+
+
+def tile_dygcn_pa_kernel(tc, A, x, out):
+    nc = tc.nc
+    with ExitStack() as ctx:
+        consts = ctx.enter_context(tc.tile_pool(name="consts", bufs=1))
+        loads = ctx.enter_context(tc.tile_pool(name="loads", bufs=GRAPHS))
+        early = ctx.enter_context(tc.tile_pool(name="early", bufs=GRAPHS))
+        small = ctx.enter_context(tc.tile_pool(name="small", bufs=2))
+        work = ctx.enter_context(tc.tile_pool(name="work", bufs=2))
+        operands = ctx.enter_context(tc.tile_pool(name="operands", bufs=2))
+        results = ctx.enter_context(tc.tile_pool(name="results", bufs=8))
+        psum_row = ctx.enter_context(tc.psum_pool(name="psum_row", bufs=1))
+        psum_flip = ctx.enter_context(tc.psum_pool(name="psum_flip", bufs=2))
+        psum_acc = ctx.enter_context(tc.psum_pool(name="psum_acc", bufs=5))
+
+        def block(i):
+            return slice(i * P, (i + 1) * P)
+
+        a_raw = []
+        x_raw = []
+        for b in range(GRAPHS):
+            a_tile = loads.tile([P, PACK, NODES], BF16, name="a_raw")
+            nc.sync.dma_start(out=a_tile[:], in_=A[b].rearrange("(t p) m -> p t m", p=P))
+            a_raw.append(a_tile)
+            x_tile = loads.tile([P, PACK, FEATS], BF16, name="x_raw")
+            nc.sync.dma_start(out=x_tile[:], in_=x[b].rearrange("(t p) f -> p t f", p=P))
+            x_raw.append(x_tile)
+
+        warm = consts.tile([P, 1], F32)
+        nc.vector.memset(warm[:], 1.0)
+        nc.scalar.activation(out=warm[:], in_=warm[:], func=ACT.Sqrt)
+        ident_f32 = consts.tile([P, P], F32)
+        make_identity(nc, ident_f32[:])
+        ident_bf16 = consts.tile([P, P], BF16)
+        make_identity(nc, ident_bf16[:])
+        eye_grouped = consts.tile([P, PACK, P, PACK], BF16)
+        nc.vector.memset(eye_grouped[:], 0.0)
+        for i in range(PACK):
+            nc.vector.tensor_copy(out=eye_grouped[:, i, :, i], in_=ident_bf16[:])
+
+        def regroup(grouped, rows):
+            nc.vector.tensor_copy(
+                out=grouped[:].rearrange("p (c i) t -> p c t i", i=4),
+                in_=rows[:].rearrange("p t (c i) -> p c t i", i=4),
+            )
+
+        def quantise(pool, grouped, name):
+            codes = pool.tile([P, NODES], U32, name=name + "_codes", align_bytes=64)
+            scales = pool.tile([P, NODES], U8, name=name + "_scales", align_bytes=64)
+            nc.vector.quantize_mx(
+                out=codes[:].bitcast(FP8X4),
+                scales=scales[:],
+                in_=grouped[:].rearrange("p w t -> p (w t)"),
+            )
+            return codes, scales
+
+        def multiply(acc, stationary, s_cols, moving, m_cols):
+            nc.tensor.matmul_mx(
+                out=acc,
+                lhsT=stationary[0][:, s_cols].bitcast(FP8X4),
+                lhsT_scale=stationary[1][:, s_cols],
+                rhs=moving[0][:, m_cols].bitcast(FP8X4),
+                rhs_scale=moving[1][:, m_cols],
+                start=True,
+                stop=True,
+            )
+
+        def product_with_x(left, x_mx, dest):
+            for c in range(PACK):
+                acc = psum_acc.tile([P, FEATS], F32, tag="acc")
+                multiply(acc[:], left, block(c), x_mx, slice(0, FEATS))
+                res = results.tile([P, FEATS], F32)
+                nc.scalar.copy(out=res[:], in_=acc[:])
+                nc.sync.dma_start(out=dest[block(c), :], in_=res[:])
+
+        x_mxs = []
+        for b in range(GRAPHS):
+            x_grouped = early.tile([P, FEATS, PACK], BF16, align_bytes=64)
+            regroup(x_grouped, x_raw[b])
+            x_mxs.append(quantise(early, x_grouped, "x"))
+
+        for b in range(GRAPHS):
+            x_mx = x_mxs[b]
+            pos = early.tile([P, PACK * DIAG_STEP], F32)
+            row_sum = early.tile([P, PACK], F32)
+            for t in range(PACK):
+                nc.scalar.activation(
+                    out=pos[:, t * NODES : (t + 1) * NODES],
+                    in_=a_raw[b][:, t, :],
+                    func=ACT.Relu,
+                    accum_out=row_sum[:, t : t + 1],
+                )
+            diagonal = pos[:].rearrange("p (t c) -> p t c", c=DIAG_STEP)[:, :, 0:P]
+            nc.vector.tensor_tensor(
+                out=diagonal,
+                in0=diagonal,
+                in1=ident_f32[:].unsqueeze(1).to_broadcast([P, PACK, P]),
+                op=ALU.add,
+            )
+
+            degree = small.tile([P, PACK], F32)
+            nc.vector.tensor_scalar(
+                out=degree[:], in0=row_sum[:], scalar1=1.0, scalar2=1e-6, op0=ALU.add, op1=ALU.max
+            )
+            root = small.tile([P, PACK], F32)
+            nc.scalar.activation(out=root[:], in_=degree[:], func=ACT.Sqrt)
+            r = small.tile([P, PACK], F32)
+            nc.vector.reciprocal(out=r[:], in_=root[:])
+
+            r_repeated = work.tile([P, PACK, P], F32)
+            nc.vector.tensor_copy(
+                out=r_repeated[:], in_=r[:].unsqueeze(2).to_broadcast([P, PACK, P])
+            )
+            r_row = psum_row.tile([P, NODES], F32)
+            for t in range(PACK):
+                nc.tensor.transpose(r_row[:, block(t)], r_repeated[:, t, :], ident_f32[:])
+
+            a_hat = work.tile([P, PACK, NODES], BF16)
+            for t in range(PACK):
+                nc.vector.scalar_tensor_tensor(
+                    out=a_hat[:, t, :],
+                    in0=pos[:, t * NODES : (t + 1) * NODES],
+                    scalar=r[:, t : t + 1],
+                    in1=r_row[:],
+                    op0=ALU.mult,
+                    op1=ALU.mult,
+                )
+
+            right_grouped = work.tile([P, NODES, PACK], BF16, align_bytes=64)
+            regroup(right_grouped, a_hat)
+            right = quantise(operands, right_grouped, "right")
+
+            left_grouped = work.tile([P, NODES, PACK], BF16, align_bytes=64)
+            for c in range(PACK):
+                flipped = psum_flip.tile([P, PACK, P], BF16)
+                for t in range(PACK):
+                    nc.tensor.transpose(flipped[:, t, :], a_hat[:, c, block(t)], ident_bf16[:])
+                nc.scalar.copy(
+                    out=left_grouped[:, block(c), :], in_=flipped[:].rearrange("p t w -> p w t")
+                )
+            left = quantise(operands, left_grouped, "left")
+
+            t2_grouped = work.tile([P, NODES, PACK], BF16, align_bytes=64)
+            for i in range(PACK):
+                acc = psum_acc.tile([P, PACK, P], F32, tag="acc")
+                for t in range(PACK):
+                    multiply(acc[:, t, :], right, block(t), left, block(i))
+                nc.vector.scalar_tensor_tensor(
+                    out=t2_grouped[:, block(i), :],
+                    in0=acc[:].rearrange("p t w -> p w t"),
+                    scalar=2.0,
+                    in1=eye_grouped[:, i, :, :],
+                    op0=ALU.mult,
+                    op1=ALU.subtract,
+                )
+            product_with_x(left, x_mx, out[b, 0])
+            t2_mx = quantise(operands, t2_grouped, "t2")
+            product_with_x(t2_mx, x_mx, out[b, 1])

@@ -26,10 +26,8 @@ def tile_dygcn_pa_kernel(tc, A, x, out):
     with ExitStack() as ctx:
         consts = ctx.enter_context(tc.tile_pool(name="consts", bufs=1))
         loads = ctx.enter_context(tc.tile_pool(name="loads", bufs=GRAPHS))
-        early = ctx.enter_context(tc.tile_pool(name="early", bufs=GRAPHS))
-        small = ctx.enter_context(tc.tile_pool(name="small", bufs=2))
+        ahead = ctx.enter_context(tc.tile_pool(name="ahead", bufs=3))
         work = ctx.enter_context(tc.tile_pool(name="work", bufs=2))
-        operands = ctx.enter_context(tc.tile_pool(name="operands", bufs=2))
         results = ctx.enter_context(tc.tile_pool(name="results", bufs=8))
         psum_row = ctx.enter_context(tc.psum_pool(name="psum_row", bufs=1))
         psum_flip = ctx.enter_context(tc.psum_pool(name="psum_flip", bufs=2))
@@ -42,7 +40,8 @@ def tile_dygcn_pa_kernel(tc, A, x, out):
         x_raw = []
         for b in range(GRAPHS):
             a_tile = loads.tile([P, PACK, NODES], BF16, name="a_raw")
-            nc.sync.dma_start(out=a_tile[:], in_=A[b].rearrange("(t p) m -> p t m", p=P))
+            for t in range(PACK):
+                nc.sync.dma_start(out=a_tile[:, t, :], in_=A[b, block(t), :])
             a_raw.append(a_tile)
             x_tile = loads.tile([P, PACK, FEATS], BF16, name="x_raw")
             nc.sync.dma_start(out=x_tile[:], in_=x[b].rearrange("(t p) f -> p t f", p=P))
@@ -66,15 +65,17 @@ def tile_dygcn_pa_kernel(tc, A, x, out):
                 in_=rows[:].rearrange("p t (c i) -> p c t i", i=4),
             )
 
-        def quantise(pool, grouped, name):
-            codes = pool.tile([P, NODES], U32, name=name + "_codes", align_bytes=64)
-            scales = pool.tile([P, NODES], U8, name=name + "_scales", align_bytes=64)
-            nc.vector.quantize_mx(
-                out=codes[:].bitcast(FP8X4),
-                scales=scales[:],
-                in_=grouped[:].rearrange("p w t -> p (w t)"),
-            )
+        def mx_tiles(name):
+            codes = work.tile([P, NODES], U32, name=name + "_codes", align_bytes=64)
+            scales = work.tile([P, NODES], U8, name=name + "_scales", align_bytes=64)
             return codes, scales
+
+        def quantise(operand, grouped, cols):
+            nc.vector.quantize_mx(
+                out=operand[0][:, cols].bitcast(FP8X4),
+                scales=operand[1][:, cols],
+                in_=grouped[:, cols, :].rearrange("p w t -> p (w t)"),
+            )
 
         def multiply(acc, stationary, s_cols, moving, m_cols):
             nc.tensor.matmul_mx(
@@ -87,94 +88,143 @@ def tile_dygcn_pa_kernel(tc, A, x, out):
                 stop=True,
             )
 
-        def product_with_x(left, x_mx, dest):
-            for c in range(PACK):
-                acc = psum_acc.tile([P, FEATS], F32, tag="acc")
-                multiply(acc[:], left, block(c), x_mx, slice(0, FEATS))
-                res = results.tile([P, FEATS], F32)
-                nc.scalar.copy(out=res[:], in_=acc[:])
-                nc.sync.dma_start(out=dest[block(c), :], in_=res[:])
+        everything = slice(0, NODES)
+        pos = {}
+        row_sum = {}
+        root = {}
+        r = {}
+        r_row = {}
+        left = {}
+        right = {}
+        x_mx = {}
+        x_grouped = {}
+        squares = {}
 
-        x_mxs = []
-        for b in range(GRAPHS):
-            x_grouped = early.tile([P, FEATS, PACK], BF16, align_bytes=64)
-            regroup(x_grouped, x_raw[b])
-            x_mxs.append(quantise(early, x_grouped, "x"))
-
-        for b in range(GRAPHS):
-            x_mx = x_mxs[b]
-            pos = early.tile([P, PACK * DIAG_STEP], F32)
-            row_sum = early.tile([P, PACK], F32)
+        def positive_part(b):
+            pos[b] = ahead.tile([P, PACK * DIAG_STEP], F32, name="pos")
+            row_sum[b] = ahead.tile([P, PACK], F32, name="row_sum")
             for t in range(PACK):
                 nc.scalar.activation(
-                    out=pos[:, t * NODES : (t + 1) * NODES],
+                    out=pos[b][:, t * NODES : (t + 1) * NODES],
                     in_=a_raw[b][:, t, :],
                     func=ACT.Relu,
-                    accum_out=row_sum[:, t : t + 1],
+                    accum_out=row_sum[b][:, t : t + 1],
                 )
-            diagonal = pos[:].rearrange("p (t c) -> p t c", c=DIAG_STEP)[:, :, 0:P]
-            nc.vector.tensor_tensor(
+            diagonal = pos[b][:].rearrange("p (t c) -> p t c", c=DIAG_STEP)[:, :, 0:P]
+            nc.gpsimd.tensor_tensor(
                 out=diagonal,
                 in0=diagonal,
                 in1=ident_f32[:].unsqueeze(1).to_broadcast([P, PACK, P]),
                 op=ALU.add,
             )
 
-            degree = small.tile([P, PACK], F32)
+        def degree_root(b):
+            degree = work.tile([P, PACK], F32)
             nc.vector.tensor_scalar(
-                out=degree[:], in0=row_sum[:], scalar1=1.0, scalar2=1e-6, op0=ALU.add, op1=ALU.max
+                out=degree[:], in0=row_sum[b][:], scalar1=1.0, scalar2=1e-6, op0=ALU.add, op1=ALU.max
             )
-            root = small.tile([P, PACK], F32)
-            nc.scalar.activation(out=root[:], in_=degree[:], func=ACT.Sqrt)
-            r = small.tile([P, PACK], F32)
-            nc.vector.reciprocal(out=r[:], in_=root[:])
+            root[b] = work.tile([P, PACK], F32, name="root")
+            nc.scalar.activation(out=root[b][:], in_=degree[:], func=ACT.Sqrt)
 
+        def scale_factors(b):
+            r[b] = work.tile([P, PACK], F32, name="r")
+            nc.vector.reciprocal(out=r[b][:], in_=root[b][:])
             r_repeated = work.tile([P, PACK, P], F32)
             nc.vector.tensor_copy(
-                out=r_repeated[:], in_=r[:].unsqueeze(2).to_broadcast([P, PACK, P])
+                out=r_repeated[:], in_=r[b][:].unsqueeze(2).to_broadcast([P, PACK, P])
             )
-            r_row = psum_row.tile([P, NODES], F32)
+            r_row[b] = psum_row.tile([P, NODES], F32, name="r_row")
             for t in range(PACK):
-                nc.tensor.transpose(r_row[:, block(t)], r_repeated[:, t, :], ident_f32[:])
+                nc.tensor.transpose(r_row[b][:, block(t)], r_repeated[:, t, :], ident_f32[:])
 
+        def normalise(b):
             a_hat = work.tile([P, PACK, NODES], BF16)
+            left_grouped = work.tile([P, NODES, PACK], BF16, align_bytes=64)
             for t in range(PACK):
                 nc.vector.scalar_tensor_tensor(
                     out=a_hat[:, t, :],
-                    in0=pos[:, t * NODES : (t + 1) * NODES],
-                    scalar=r[:, t : t + 1],
-                    in1=r_row[:],
+                    in0=pos[b][:, t * NODES : (t + 1) * NODES],
+                    scalar=r[b][:, t : t + 1],
+                    in1=r_row[b][:],
                     op0=ALU.mult,
                     op1=ALU.mult,
                 )
+                flipped = psum_flip.tile([P, PACK, P], BF16)
+                for u in range(PACK):
+                    nc.tensor.transpose(flipped[:, u, :], a_hat[:, t, block(u)], ident_bf16[:])
+                nc.scalar.copy(
+                    out=left_grouped[:, block(t), :], in_=flipped[:].rearrange("p u w -> p w u")
+                )
+            return a_hat, left_grouped
 
+        def product_with_x(b, which, operand, c):
+            acc = psum_acc.tile([P, FEATS], F32, tag="acc", name="product")
+            multiply(acc[:], operand, block(c), x_mx[b], everything)
+            res = results.tile([P, FEATS], F32)
+            nc.scalar.copy(out=res[:], in_=acc[:])
+            nc.sync.dma_start(out=out[b, which, block(c), :], in_=res[:])
+
+        def regroup_x(b):
+            x_grouped[b] = work.tile([P, FEATS, PACK], BF16, name="x_grouped", align_bytes=64)
+            regroup(x_grouped[b], x_raw[b])
+
+        def quantise_x(b):
+            x_mx[b] = mx_tiles("x")
+            quantise(x_mx[b], x_grouped[b], everything)
+
+        def make_operands(b, a_hat, left_grouped):
             right_grouped = work.tile([P, NODES, PACK], BF16, align_bytes=64)
             regroup(right_grouped, a_hat)
-            right = quantise(operands, right_grouped, "right")
-
-            left_grouped = work.tile([P, NODES, PACK], BF16, align_bytes=64)
+            left[b] = mx_tiles("left")
+            quantise(left[b], left_grouped, everything)
             for c in range(PACK):
-                flipped = psum_flip.tile([P, PACK, P], BF16)
-                for t in range(PACK):
-                    nc.tensor.transpose(flipped[:, t, :], a_hat[:, c, block(t)], ident_bf16[:])
-                nc.scalar.copy(
-                    out=left_grouped[:, block(c), :], in_=flipped[:].rearrange("p t w -> p w t")
-                )
-            left = quantise(operands, left_grouped, "left")
-
-            t2_grouped = work.tile([P, NODES, PACK], BF16, align_bytes=64)
+                product_with_x(b, 0, left[b], c)
+            if b + 1 < GRAPHS:
+                regroup_x(b + 1)
+            right[b] = mx_tiles("right")
+            quantise(right[b], right_grouped, everything)
+            if b + 1 < GRAPHS:
+                quantise_x(b + 1)
+            squares[b] = []
             for i in range(PACK):
-                acc = psum_acc.tile([P, PACK, P], F32, tag="acc")
+                acc = psum_acc.tile([P, PACK, P], F32, tag="acc", name="square")
                 for t in range(PACK):
-                    multiply(acc[:, t, :], right, block(t), left, block(i))
-                nc.vector.scalar_tensor_tensor(
-                    out=t2_grouped[:, block(i), :],
-                    in0=acc[:].rearrange("p t w -> p w t"),
-                    scalar=2.0,
-                    in1=eye_grouped[:, i, :, :],
-                    op0=ALU.mult,
-                    op1=ALU.subtract,
-                )
-            product_with_x(left, x_mx, out[b, 0])
-            t2_mx = quantise(operands, t2_grouped, "t2")
-            product_with_x(t2_mx, x_mx, out[b, 1])
+                    multiply(acc[:, t, :], right[b], block(t), left[b], block(i))
+                squares[b].append(acc)
+
+        def products(b):
+            t2_grouped = work.tile([P, NODES, PACK], BF16, align_bytes=64)
+            t2_mx = mx_tiles("t2")
+            for i in range(PACK + 1):
+                if i < PACK:
+                    nc.vector.scalar_tensor_tensor(
+                        out=t2_grouped[:, block(i), :],
+                        in0=squares[b][i][:].rearrange("p t w -> p w t"),
+                        scalar=2.0,
+                        in1=eye_grouped[:, i, :, :],
+                        op0=ALU.mult,
+                        op1=ALU.subtract,
+                    )
+                if i >= 1:
+                    quantise(t2_mx, t2_grouped, block(i - 1))
+                    product_with_x(b, 1, t2_mx, i - 1)
+
+        positive_part(0)
+        regroup_x(0)
+        degree_root(0)
+        scale_factors(0)
+        quantise_x(0)
+        positive_part(1)
+        for b in range(GRAPHS + 1):
+            if b < GRAPHS:
+                a_hat, left_grouped = normalise(b)
+            if b + 1 < GRAPHS:
+                degree_root(b + 1)
+            if b >= 1:
+                products(b - 1)
+            if b + 1 < GRAPHS:
+                scale_factors(b + 1)
+            if b < GRAPHS:
+                make_operands(b, a_hat, left_grouped)
+            if b + 2 < GRAPHS:
+                positive_part(b + 2)

@@ -129,13 +129,11 @@ def tile_dygcn_pa_kernel(tc, A, x, out):
         def scale_factors(b):
             r[b] = work.tile([P, PACK], F32, name="r")
             nc.vector.reciprocal(out=r[b][:], in_=root[b][:])
-            r_repeated = work.tile([P, PACK, P], F32)
-            nc.vector.tensor_copy(
-                out=r_repeated[:], in_=r[b][:].unsqueeze(2).to_broadcast([P, PACK, P])
-            )
             r_row[b] = psum_row.tile([P, NODES], F32, name="r_row")
             for t in range(PACK):
-                nc.tensor.transpose(r_row[b][:, block(t)], r_repeated[:, t, :], ident_f32[:])
+                nc.tensor.transpose(
+                    r_row[b][:, block(t)], r[b][:, t : t + 1].to_broadcast([P, P]), ident_f32[:]
+                )
 
         def normalise(b):
             a_hat = work.tile([P, PACK, NODES], BF16)

@@ -119,16 +119,14 @@ def tile_dygcn_pa_kernel(tc, A, x, out):
             )
 
         def degree_root(b):
-            degree = work.tile([P, PACK], F32)
-            nc.vector.tensor_scalar(
-                out=degree[:], in0=row_sum[b][:], scalar1=1.0, scalar2=1e-6, op0=ALU.add, op1=ALU.max
-            )
             root[b] = work.tile([P, PACK], F32, name="root")
-            nc.scalar.activation(out=root[b][:], in_=degree[:], func=ACT.Sqrt)
+            nc.scalar.activation(out=root[b][:], in_=row_sum[b][:], func=ACT.Sqrt, bias=1.0)
 
         def scale_factors(b):
+            bounded = work.tile([P, PACK], F32)
+            nc.vector.tensor_scalar_max(out=bounded[:], in0=root[b][:], scalar1=1e-3)
             r[b] = work.tile([P, PACK], F32, name="r")
-            nc.vector.reciprocal(out=r[b][:], in_=root[b][:])
+            nc.vector.reciprocal(out=r[b][:], in_=bounded[:])
             r_row[b] = psum_row.tile([P, NODES], F32, name="r_row")
             for t in range(PACK):
                 nc.tensor.transpose(
@@ -163,8 +161,16 @@ def tile_dygcn_pa_kernel(tc, A, x, out):
             nc.sync.dma_start(out=out[b, which, block(c), :], in_=res[:])
 
         def regroup_x(b):
-            x_grouped[b] = work.tile([P, FEATS, PACK], BF16, name="x_grouped", align_bytes=64)
-            regroup(x_grouped[b], x_raw[b])
+            x_grouped[b] = loads.tile([P, FEATS, PACK], BF16, name="x_grouped", align_bytes=64)
+            for c in range(PACK):
+                nc.gpsimd.tensor_scalar(
+                    out=x_grouped[b][:, block(c), :],
+                    in0=x_raw[b][:, :, block(c)].rearrange("p t f -> p f t"),
+                    scalar1=1.0,
+                    scalar2=0.0,
+                    op0=ALU.mult,
+                    op1=ALU.add,
+                )
 
         def quantise_x(b):
             x_mx[b] = mx_tiles("x")

from contextlib import ExitStack

import concourse.mybir as mybir
from concourse.masks import make_identity

BF16 = mybir.dt.bfloat16
F32 = mybir.dt.float32
U32 = mybir.dt.uint32
U8 = mybir.dt.uint8
FP8X4 = mybir.dt.float8_e4m3fn_x4
ACT = mybir.ActivationFunctionType
ALU = mybir.AluOpType

P = 128
PACK = 4
GRAPHS = 4
NODES = P * PACK
FEATS = 512
DIAG_STEP = NODES + P

FLOPS = 3 * GRAPHS * 2 * NODES * NODES * FEATS


def tile_dygcn_pa_kernel(tc, A, x, out):
    nc = tc.nc
    with ExitStack() as ctx:
        consts = ctx.enter_context(tc.tile_pool(name="consts", bufs=1))
        loads = ctx.enter_context(tc.tile_pool(name="loads", bufs=GRAPHS))
        ahead = ctx.enter_context(tc.tile_pool(name="ahead", bufs=3))
        work = ctx.enter_context(tc.tile_pool(name="work", bufs=2))
        results = ctx.enter_context(tc.tile_pool(name="results", bufs=8))
        psum_row = ctx.enter_context(tc.psum_pool(name="psum_row", bufs=1))
        psum_flip = ctx.enter_context(tc.psum_pool(name="psum_flip", bufs=2))
        psum_acc = ctx.enter_context(tc.psum_pool(name="psum_acc", bufs=5))

        def block(i):
            return slice(i * P, (i + 1) * P)

        a_raw = []
        x_raw = []
        for b in range(GRAPHS):
            a_tile = loads.tile([P, PACK, NODES], BF16, name="a_raw")
            for t in range(PACK):
                nc.sync.dma_start(out=a_tile[:, t, :], in_=A[b, block(t), :])
            a_raw.append(a_tile)
            x_tile = loads.tile([P, PACK, FEATS], BF16, name="x_raw")
            nc.sync.dma_start(out=x_tile[:], in_=x[b].rearrange("(t p) f -> p t f", p=P))
            x_raw.append(x_tile)

        warm = consts.tile([P, 1], F32)
        nc.vector.memset(warm[:], 1.0)
        nc.scalar.activation(out=warm[:], in_=warm[:], func=ACT.Sqrt)
        ident_f32 = consts.tile([P, P], F32)
        make_identity(nc, ident_f32[:])
        ident_bf16 = consts.tile([P, P], BF16)
        make_identity(nc, ident_bf16[:])
        eye_grouped = consts.tile([P, PACK, P, PACK], BF16)
        nc.vector.memset(eye_grouped[:], 0.0)
        for i in range(PACK):
            nc.vector.tensor_copy(out=eye_grouped[:, i, :, i], in_=ident_bf16[:])

        def regroup(grouped, rows):
            nc.vector.tensor_copy(
                out=grouped[:].rearrange("p (c i) t -> p c t i", i=4),
                in_=rows[:].rearrange("p t (c i) -> p c t i", i=4),
            )

        def mx_tiles(name):
            codes = work.tile([P, NODES], U32, name=name + "_codes", align_bytes=64)
            scales = work.tile([P, NODES], U8, name=name + "_scales", align_bytes=64)
            return codes, scales

        def quantise(operand, grouped, cols):
            nc.vector.quantize_mx(
                out=operand[0][:, cols].bitcast(FP8X4),
                scales=operand[1][:, cols],
                in_=grouped[:, cols, :].rearrange("p w t -> p (w t)"),
            )

        def multiply(acc, stationary, s_cols, moving, m_cols):
            nc.tensor.matmul_mx(
                out=acc,
                lhsT=stationary[0][:, s_cols].bitcast(FP8X4),
                lhsT_scale=stationary[1][:, s_cols],
                rhs=moving[0][:, m_cols].bitcast(FP8X4),
                rhs_scale=moving[1][:, m_cols],
                start=True,
                stop=True,
            )

        everything = slice(0, NODES)
        pos = {}
        row_sum = {}
        root = {}
        r = {}
        r_row = {}
        left = {}
        right = {}
        x_mx = {}
        x_grouped = {}
        squares = {}

        def positive_part(b):
            pos[b] = ahead.tile([P, PACK * DIAG_STEP], F32, name="pos")
            row_sum[b] = ahead.tile([P, PACK], F32, name="row_sum")
            for t in range(PACK):
                nc.scalar.activation(
                    out=pos[b][:, t * NODES : (t + 1) * NODES],
                    in_=a_raw[b][:, t, :],
                    func=ACT.Relu,
                    accum_out=row_sum[b][:, t : t + 1],
                )
            diagonal = pos[b][:].rearrange("p (t c) -> p t c", c=DIAG_STEP)[:, :, 0:P]
            nc.gpsimd.tensor_tensor(
                out=diagonal,
                in0=diagonal,
                in1=ident_f32[:].unsqueeze(1).to_broadcast([P, PACK, P]),
                op=ALU.add,
            )

        def degree_root(b):
            root[b] = work.tile([P, PACK], F32, name="root")
            nc.scalar.activation(out=root[b][:], in_=row_sum[b][:], func=ACT.Sqrt, bias=1.0)

        def scale_factors(b):
            bounded = work.tile([P, PACK], F32)
            nc.vector.tensor_scalar_max(out=bounded[:], in0=root[b][:], scalar1=1e-3)
            r[b] = work.tile([P, PACK], F32, name="r")
            nc.vector.reciprocal(out=r[b][:], in_=bounded[:])
            r_row[b] = psum_row.tile([P, NODES], F32, name="r_row")
            for t in range(PACK):
                nc.tensor.transpose(
                    r_row[b][:, block(t)], r[b][:, t : t + 1].to_broadcast([P, P]), ident_f32[:]
                )

        def normalise(b):
            a_hat = work.tile([P, PACK, NODES], BF16)
            left_grouped = work.tile([P, NODES, PACK], BF16, align_bytes=64)
            for t in range(PACK):
                nc.vector.scalar_tensor_tensor(
                    out=a_hat[:, t, :],
                    in0=pos[b][:, t * NODES : (t + 1) * NODES],
                    scalar=r[b][:, t : t + 1],
                    in1=r_row[b][:],
                    op0=ALU.mult,
                    op1=ALU.mult,
                )
                flipped = psum_flip.tile([P, PACK, P], BF16)
                for u in range(PACK):
                    nc.tensor.transpose(flipped[:, u, :], a_hat[:, t, block(u)], ident_bf16[:])
                nc.scalar.copy(
                    out=left_grouped[:, block(t), :], in_=flipped[:].rearrange("p u w -> p w u")
                )
            return a_hat, left_grouped

        def product_with_x(b, which, operand, c):
            acc = psum_acc.tile([P, FEATS], F32, tag="acc", name="product")
            multiply(acc[:], operand, block(c), x_mx[b], everything)
            res = results.tile([P, FEATS], F32)
            nc.scalar.copy(out=res[:], in_=acc[:])
            nc.sync.dma_start(out=out[b, which, block(c), :], in_=res[:])

        def regroup_x(b):
            x_grouped[b] = loads.tile([P, FEATS, PACK], BF16, name="x_grouped", align_bytes=64)
            for c in range(PACK):
                nc.gpsimd.tensor_scalar(
                    out=x_grouped[b][:, block(c), :],
                    in0=x_raw[b][:, :, block(c)].rearrange("p t f -> p f t"),
                    scalar1=1.0,
                    scalar2=0.0,
                    op0=ALU.mult,
                    op1=ALU.add,
                )

        def quantise_x(b):
            x_mx[b] = mx_tiles("x")
            quantise(x_mx[b], x_grouped[b], everything)

        def make_operands(b, a_hat, left_grouped):
            right_grouped = work.tile([P, NODES, PACK], BF16, align_bytes=64)
            regroup(right_grouped, a_hat)
            left[b] = mx_tiles("left")
            quantise(left[b], left_grouped, everything)
            for c in range(PACK):
                product_with_x(b, 0, left[b], c)
            if b + 1 < GRAPHS:
                regroup_x(b + 1)
            right[b] = mx_tiles("right")
            quantise(right[b], right_grouped, everything)
            if b + 1 < GRAPHS:
                quantise_x(b + 1)
            squares[b] = []
            for i in range(PACK):
                acc = psum_acc.tile([P, PACK, P], F32, tag="acc", name="square")
                for t in range(PACK):
                    multiply(acc[:, t, :], right[b], block(t), left[b], block(i))
                squares[b].append(acc)

        def products(b):
            t2_grouped = work.tile([P, NODES, PACK], BF16, align_bytes=64)
            t2_mx = mx_tiles("t2")
            for i in range(PACK + 1):
                if i < PACK:
                    nc.vector.scalar_tensor_tensor(
                        out=t2_grouped[:, block(i), :],
                        in0=squares[b][i][:].rearrange("p t w -> p w t"),
                        scalar=2.0,
                        in1=eye_grouped[:, i, :, :],
                        op0=ALU.mult,
                        op1=ALU.subtract,
                    )
                if i >= 1:
                    quantise(t2_mx, t2_grouped, block(i - 1))
                    product_with_x(b, 1, t2_mx, i - 1)

        positive_part(0)
        regroup_x(0)
        degree_root(0)
        scale_factors(0)
        quantise_x(0)
        positive_part(1)
        for b in range(GRAPHS + 1):
            if b < GRAPHS:
                a_hat, left_grouped = normalise(b)
            if b + 1 < GRAPHS:
                degree_root(b + 1)
            if b >= 1:
                products(b - 1)
            if b + 1 < GRAPHS:
                scale_factors(b + 1)
            if b < GRAPHS:
                make_operands(b, a_hat, left_grouped)
            if b + 2 < GRAPHS:
                positive_part(b + 2)
